import numpy as np
import ml_dtypes


def mxq(x, axis, fmt="e4m3"):
    dtype, down = {"e4m3": (ml_dtypes.float8_e4m3fn, 7), "e5m2": (ml_dtypes.float8_e5m2, 14)}[fmt]
    v = np.moveaxis(np.asarray(x, np.float32).astype(ml_dtypes.bfloat16).astype(np.float64), axis, -1)
    blocks = v.reshape(v.shape[:-1] + (-1, 32))
    amax = np.abs(blocks).max(-1, keepdims=True)
    byte = np.maximum(np.where(amax > 0, np.frexp(amax)[1] - 1 + 127, 0) - down, 1)
    scale = np.exp2(byte - 127.0)
    codes = (blocks / scale).astype(np.float32).astype(dtype).astype(np.float64)
    return np.moveaxis((codes * scale).reshape(v.shape), -1, axis)


WIDE = False


def mx_kscale(k):
    if not WIDE:
        return np.ones(k)
    levels = np.array([10, -10, 5, -5, 0])
    a = np.random.permutation(np.resize(levels, k // 512 * 4)).reshape(k // 512, 4)
    idx = np.arange(k)
    return np.exp2(a[idx // 512, idx % 128 // 32])


BF16 = ml_dtypes.bfloat16


def bf(x):
    return np.asarray(x, np.float32).astype(BF16)


def f64(x):
    return np.asarray(x).astype(np.float64)


B, S, E, H, D, F = 4, 2048, 1024, 2, 64, 4096
EPS = 1e-6
QUIET = 1e-3


def rmsnorm(x, scale):
    ms = np.mean(np.square(x), axis=-1, keepdims=True)
    return x * (1.0 / np.sqrt(ms + EPS)) * scale


def setup_inputs():
    s = mx_kscale(E)
    amp = np.where(np.random.random((B, S, 1)) < 0.25, QUIET, 1.0)
    return {"x": bf(np.random.standard_normal((B, S, E)) * amp),
            "scale1": bf(np.random.standard_normal(E) * s),
            "w_qkv": bf(np.random.standard_normal((E, H, 3 * D)) / np.sqrt(E) / s[:, None, None])}


def reference(x, scale1, w_qkv):
    xn = rmsnorm(f64(x), f64(scale1)).reshape(B * S, E)
    qkv = (mxq(xn, 1, "e4m3") @ mxq(f64(w_qkv).reshape(E, H * 3 * D), 0, "e4m3")).reshape(B, S, H, 3 * D)
    q, k, v = np.split(qkv, 3, axis=-1)
    return q, k, v

@@ -1,0 +1,318 @@
+from contextlib import ExitStack
+
+import concourse.mybir as mybir
+from concourse.masks import make_identity
+
+F32 = mybir.dt.float32
+BF16 = mybir.dt.bfloat16
+U32 = mybir.dt.uint32
+U8 = mybir.dt.uint8
+FP8X4 = mybir.dt.float8_e4m3fn_x4
+ACT = mybir.ActivationFunctionType
+ALU = mybir.AluOpType
+
+P = 128
+ROWS = 4 * 2048
+E = 1024
+HEADS = 2
+PARTS = 3
+D = 64
+COLS = HEADS * PARTS * D
+EPS = 1e-6
+
+PACK = 4
+PASSES = E // (P * PACK)
+WORDS = E // 2
+BLOCKS = WORDS // P
+
+TILES = 4
+GROUP_ROWS = P * TILES
+GROUPS = ROWS // GROUP_ROWS
+
+PART_COLS = HEADS * D
+QK_COLS = 2 * PART_COLS
+COLUMN_CUTS = ((0, QK_COLS), (QK_COLS, COLS))
+BANK = 512
+
+GPSIMD_COLS = E + E // 4
+VECTOR_COLS = TILES * E - GPSIMD_COLS
+VECTOR_BANK = TILES - 1
+SUMS_LAG = 2
+
+FLOPS = 2 * ROWS * E * COLS
+
+
+def vector_share(j):
+    return min(E, max(0, VECTOR_COLS - j * E))
+
+
+def tile_block_pa_t_kernel(tc, x, scale1, w_qkv, out_0, out_1, out_2):
+    nc = tc.nc
+
+    x_groups = x.rearrange("b s e -> (b s) e").rearrange(
+        "(n p j) e -> n p (j e)", p=P, j=TILES
+    )
+    out_groups = [
+        out.rearrange("b s h d -> (b s) (h d)").rearrange(
+            "(n p j) c -> n p (j c)", p=P, j=TILES
+        )
+        for out in (out_0, out_1, out_2)
+    ]
+
+    with ExitStack() as ctx:
+        const = ctx.enter_context(tc.tile_pool(name="const", bufs=1))
+        x_pool = ctx.enter_context(tc.tile_pool(name="x_pool", bufs=GROUPS))
+        stat_pool = ctx.enter_context(tc.tile_pool(name="stat_pool", bufs=4))
+        square_pool = ctx.enter_context(tc.tile_pool(name="square_pool", bufs=4))
+        work = ctx.enter_context(tc.tile_pool(name="work", bufs=2))
+        out_pool = ctx.enter_context(tc.tile_pool(name="out_pool", bufs=3))
+        gain_psum = ctx.enter_context(tc.psum_pool(name="gain_psum", bufs=1))
+        turned_psum = ctx.enter_context(tc.psum_pool(name="turned_psum", bufs=TILES))
+        acc_psum = ctx.enter_context(tc.psum_pool(name="acc_psum", bufs=3))
+        ctx.enter_context(tc.manual_schedule())
+
+        x_tiles = [x_pool.tile([P, TILES, E], BF16, name="x_sb") for n in range(GROUPS)]
+
+        def load_x(n, first_tile, tiles):
+            c0, c1 = first_tile * E, (first_tile + tiles) * E
+            nc.sync.dma_start(
+                out=x_tiles[n][:].rearrange("p j e -> p (j e)")[:, c0:c1], in_=x_groups[n][:, c0:c1]
+            )
+
+        w_raw = const.tile([P, PASSES, PACK, COLS], BF16)
+        w_passes = w_qkv.rearrange("k h c -> k (h c)").rearrange(
+            "(g u p e) c -> g p u (e c)", g=PASSES, p=P, e=2
+        )
+
+        def load_w(g):
+            nc.sync.dma_start(
+                out=w_raw[:, g].rearrange("p (u e) c -> p u (e c)", e=2), in_=w_passes[g]
+            )
+
+        gain_row = const.tile([P, E], BF16)
+        nc.vector.memset(gain_row[:], 0.0)
+
+        load_x(0, 0, 1)
+        nc.sync.dma_start(out=gain_row[0:1, :], in_=scale1.unsqueeze(0))
+        load_x(0, 1, 1)
+        load_w(0)
+        load_x(0, 2, 1)
+        load_w(1)
+        load_x(0, 3, 1)
+        for n in range(1, GROUPS):
+            load_x(n, 0, TILES)
+
+        ident = const.tile([P, P], F32)
+        make_identity(nc, ident[:])
+        ones = const.tile([P, P], BF16)
+        nc.vector.memset(ones[:], 1.0)
+        warm = const.tile([P, 1], F32)
+        nc.vector.memset(warm[:], 1.0)
+        nc.scalar.activation(out=warm[:], in_=warm[:], func=ACT.Sqrt)
+
+        gain_bank = gain_psum.tile([P, E], BF16)
+        gpsimd_gain = const.tile([P, GPSIMD_COLS], BF16)
+
+        def spread_gain():
+            for c0 in range(0, E, BANK):
+                nc.tensor.matmul(
+                    out=gain_bank[:, c0 : c0 + BANK],
+                    lhsT=ones[:],
+                    rhs=gain_row[:, c0 : c0 + BANK],
+                    start=True,
+                    stop=True,
+                )
+            nc.vector.tensor_copy(
+                out=gpsimd_gain[:, : GPSIMD_COLS - E], in_=gain_bank[:, 2 * E - GPSIMD_COLS :]
+            )
+            nc.vector.tensor_copy(out=gpsimd_gain[:, GPSIMD_COLS - E :], in_=gain_bank[:])
+
+        w_grouped = const.tile([P, PASSES, COLS, PACK], BF16, align_bytes=64)
+        w_codes = const.tile([P, PASSES, COLS], U32, align_bytes=64)
+        w_scales = const.tile([P, PASSES, COLS], U8, align_bytes=64)
+
+        def regroup_weights(g):
+            by_part = w_raw[:, g].rearrange("p t (h s d) -> p s h d t", h=HEADS, s=PARTS)
+            for s in range(PARTS):
+                nc.vector.tensor_copy(
+                    out=w_grouped[:, g, s * PART_COLS : (s + 1) * PART_COLS, :].rearrange(
+                        "p (h d) t -> p h d t", h=HEADS
+                    ),
+                    in_=by_part[:, s],
+                )
+
+        def quantise_weights():
+            for g in range(PASSES):
+                for c0, c1 in COLUMN_CUTS:
+                    nc.vector.quantize_mx(
+                        out=w_codes[:, g, c0:c1].bitcast(FP8X4),
+                        scales=w_scales[:, g, c0:c1],
+                        in_=w_grouped[:, g, c0:c1, :].rearrange("p c t -> p (c t)"),
+                    )
+
+        sum_sq_of, rms_of, rstd_of, scaled_of, turned_of = {}, {}, {}, {}, {}
+        grouped_of, codes_of, scales_of, acc_of = {}, {}, {}, {}
+
+        def in_range(n):
+            return 0 <= n < GROUPS
+
+        def sum_squares(n):
+            sum_sq = stat_pool.tile([P, TILES], F32, name="sum_sq")
+            for j in range(TILES):
+                squares = square_pool.tile([P, E], BF16, name="squares")
+                nc.scalar.activation(
+                    out=squares[:],
+                    in_=x_tiles[n][:, j, :],
+                    func=ACT.Square,
+                    accum_out=sum_sq[:, j : j + 1],
+                )
+            sum_sq_of[n] = sum_sq
+
+        def root(n):
+            rms = stat_pool.tile([P, TILES], F32, name="rms")
+            nc.scalar.activation(
+                out=rms[:], in_=sum_sq_of[n][:], func=ACT.Sqrt, scale=1.0 / E, bias=EPS
+            )
+            rms_of[n] = rms
+
+        def invert(n):
+            rstd = stat_pool.tile([P, TILES], F32, name="rstd")
+            nc.vector.reciprocal(rstd[:], rms_of[n][:])
+            rstd_of[n] = rstd
+
+        def gpsimd_scale(n):
+            scaled = work.tile([P, GPSIMD_COLS], F32, name="scaled")
+            nc.gpsimd.tensor_tensor(
+                out=scaled[:],
+                in0=x_tiles[n][:].rearrange("p j e -> p (j e)")[:, VECTOR_COLS:],
+                in1=gpsimd_gain[:],
+                op=ALU.mult,
+            )
+            scaled_of[n] = scaled
+
+        def normalise_and_turn(n):
+            xn = work.tile([P, TILES, E], BF16, name="xn")
+            xn_words = xn[:].bitcast(F32)
+            for j in range(TILES):
+                first = vector_share(j)
+                if first < E:
+                    start = j * E + first - VECTOR_COLS
+                    nc.gpsimd.tensor_scalar(
+                        out=xn[:, j, first:],
+                        in0=scaled_of[n][:, start : start + E - first],
+                        scalar1=rstd_of[n][:, j : j + 1],
+                        scalar2=0.0,
+                        op0=ALU.mult,
+                        op1=ALU.add,
+                    )
+            turned_of[n] = []
+            for j in range(TILES):
+                share = vector_share(j)
+                if share > 0:
+                    nc.vector.scalar_tensor_tensor(
+                        out=xn[:, j, :share],
+                        in0=x_tiles[n][:, j, :share],
+                        scalar=rstd_of[n][:, j : j + 1],
+                        in1=gain_bank[:, :share],
+                        op0=ALU.mult,
+                        op1=ALU.mult,
+                    )
+                turned = turned_psum.tile([P, BLOCKS, P], F32, name="turned")
+                for b in range(BLOCKS):
+                    nc.tensor.transpose(
+                        turned[:, b, :], xn_words[:, j, b * P : (b + 1) * P], ident[:]
+                    )
+                turned_of[n].append(turned)
+            grouped_of[n] = work.tile(
+                [P, TILES, PASSES, P, PACK], BF16, align_bytes=64, name="grouped"
+            )
+
+        def copy_turned(n, j):
+            copy = nc.vector.tensor_copy if j == VECTOR_BANK or n < SUMS_LAG else nc.scalar.copy
+            copy(
+                out=grouped_of[n][:].bitcast(F32)[:, j],
+                in_=turned_of[n][j][:].rearrange("p (g u) r -> p g r u", u=2),
+            )
+
+        def quantise(n):
+            codes = work.tile([P, TILES, PASSES, P], U32, align_bytes=64, name="codes")
+            scales = work.tile([P, TILES, PASSES, P], U8, align_bytes=64, name="scales")
+            nc.vector.quantize_mx(
+                out=codes[:].rearrange("p j g r -> p (j g r)").bitcast(FP8X4),
+                scales=scales[:].rearrange("p j g r -> p (j g r)"),
+                in_=grouped_of[n][:].rearrange("p j g r t -> p (j g r t)"),
+            )
+            codes_of[n] = codes
+            scales_of[n] = scales
+
+        def multiply(n, j, c0, c1, out):
+            for g in range(PASSES):
+                nc.tensor.matmul_mx(
+                    out=out,
+                    lhsT=codes_of[n][:, j, g, :].bitcast(FP8X4),
+                    lhsT_scale=scales_of[n][:, j, g, :],
+                    rhs=w_codes[:, g, c0:c1].bitcast(FP8X4),
+                    rhs_scale=w_scales[:, g, c0:c1],
+                    start=(g == 0),
+                    stop=(g == PASSES - 1),
+                )
+
+        def project(n):
+            qk_banks = []
+            for first in range(0, TILES, 2):
+                qk = acc_psum.tile([P, 2, QK_COLS], F32, name="acc")
+                for i in range(2):
+                    multiply(n, first + i, 0, QK_COLS, qk[:, i, :])
+                qk_banks.append(qk)
+            v_bank = acc_psum.tile([P, TILES, PART_COLS], F32, name="acc")
+            for j in range(TILES):
+                multiply(n, j, QK_COLS, COLS, v_bank[:, j, :])
+            acc_of[n] = (qk_banks, v_bank)
+
+        def copy_and_store(n):
+            copy = nc.vector.tensor_copy if in_range(n + SUMS_LAG + 2) else nc.scalar.copy
+            qk_banks, v_bank = acc_of[n]
+            result = out_pool.tile([P, PARTS, TILES, PART_COLS], F32, name="result")
+            for i, qk in enumerate(qk_banks):
+                copy(
+                    out=result[:, 0:2, 2 * i : 2 * i + 2, :],
+                    in_=qk[:].rearrange("p j (s c) -> p s j c", s=2),
+                )
+            copy(out=result[:, 2], in_=v_bank[:])
+            for s in range(PARTS):
+                nc.sync.dma_start(
+                    out=out_groups[s][n], in_=result[:, s].rearrange("p j c -> p (j c)")
+                )
+
+        sum_squares(0)
+        root(0)
+        sum_squares(1)
+        regroup_weights(0)
+        spread_gain()
+        regroup_weights(1)
+        quantise_weights()
+        invert(0)
+        gpsimd_scale(0)
+
+        for r in range(GROUPS + SUMS_LAG):
+            if in_range(r - 1):
+                copy_turned(r - 1, VECTOR_BANK)
+            if in_range(r):
+                normalise_and_turn(r)
+                copy_turned(r, 0)
+            if in_range(r + 1):
+                root(r + 1)
+            if in_range(r - 1):
+                quantise(r - 1)
+            if in_range(r + 1):
+                invert(r + 1)
+                gpsimd_scale(r + 1)
+            if in_range(r):
+                for j in range(1, VECTOR_BANK):
+                    copy_turned(r, j)
+            if in_range(r - SUMS_LAG):
+                copy_and_store(r - SUMS_LAG)
+            if in_range(r - 1):
+                project(r - 1)
+            if in_range(r + 2):
+                sum_squares(r + 2)

@@ -156,17 +156,19 @@ def tile_block_pa_t_kernel(tc, x, scale1, w_qkv, out_0, out_1, out_2):
         def in_range(n):
             return 0 <= n < GROUPS
 
+        def square_tile(n, j):
+            squares = square_pool.tile([P, E], BF16, name="squares")
+            nc.scalar.activation(
+                out=squares[:],
+                in_=x_tiles[n][:, j, :],
+                func=ACT.Square,
+                accum_out=sum_sq_of[n][:, j : j + 1],
+            )
+
         def sum_squares(n):
-            sum_sq = stat_pool.tile([P, TILES], F32, name="sum_sq")
+            sum_sq_of[n] = stat_pool.tile([P, TILES], F32, name="sum_sq")
             for j in range(TILES):
-                squares = square_pool.tile([P, E], BF16, name="squares")
-                nc.scalar.activation(
-                    out=squares[:],
-                    in_=x_tiles[n][:, j, :],
-                    func=ACT.Square,
-                    accum_out=sum_sq[:, j : j + 1],
-                )
-            sum_sq_of[n] = sum_sq
+                square_tile(n, j)
 
         def root(n):
             rms = stat_pool.tile([P, TILES], F32, name="rms")
@@ -307,12 +309,14 @@ def tile_block_pa_t_kernel(tc, x, scale1, w_qkv, out_0, out_1, out_2):
             if in_range(r + 1):
                 invert(r + 1)
                 gpsimd_scale(r + 1)
-            if in_range(r):
-                for j in range(1, VECTOR_BANK):
+            if in_range(r + 2):
+                sum_sq_of[r + 2] = stat_pool.tile([P, TILES], F32, name="sum_sq")
+            for j in range(TILES):
+                if in_range(r) and 1 <= j < VECTOR_BANK:
                     copy_turned(r, j)
+                if in_range(r + 2):
+                    square_tile(r + 2, j)
             if in_range(r - SUMS_LAG):
                 copy_and_store(r - SUMS_LAG)
             if in_range(r - 1):
                 project(r - 1)
-            if in_range(r + 2):
-                sum_squares(r + 2)

@@ -42,8 +42,8 @@ SUMS_LAG = 2
 FLOPS = 2 * ROWS * E * COLS
 
 
-def vector_share(j):
-    return min(E, max(0, VECTOR_COLS - j * E))
+def vector_share(n, j):
+    return E if n == 0 else min(E, max(0, VECTOR_COLS - j * E))
 
 
 def tile_block_pa_t_kernel(tc, x, scale1, w_qkv, out_0, out_1, out_2):
@@ -94,12 +94,13 @@ def tile_block_pa_t_kernel(tc, x, scale1, w_qkv, out_0, out_1, out_2):
 
         load_x(0, 0, 1)
         nc.sync.dma_start(out=gain_row[0:1, :], in_=scale1.unsqueeze(0))
-        load_x(0, 1, 1)
+        for j in range(1, TILES):
+            load_x(0, j, 1)
+        load_x(1, 0, 2)
+        load_x(1, 2, 2)
         load_w(0)
-        load_x(0, 2, 1)
         load_w(1)
-        load_x(0, 3, 1)
-        for n in range(1, GROUPS):
+        for n in range(2, GROUPS):
             load_x(n, 0, TILES)
 
         ident = const.tile([P, P], F32)
@@ -151,7 +152,7 @@ def tile_block_pa_t_kernel(tc, x, scale1, w_qkv, out_0, out_1, out_2):
                     )
 
         sum_sq_of, rms_of, rstd_of, scaled_of, turned_of = {}, {}, {}, {}, {}
-        grouped_of, codes_of, scales_of, acc_of = {}, {}, {}, {}
+        grouped_of, codes_of, scales_of, acc_of, xn_of, result_of = {}, {}, {}, {}, {}, {}
 
         def in_range(n):
             return 0 <= n < GROUPS
@@ -170,17 +171,23 @@ def tile_block_pa_t_kernel(tc, x, scale1, w_qkv, out_0, out_1, out_2):
             for j in range(TILES):
                 square_tile(n, j)
 
-        def root(n):
-            rms = stat_pool.tile([P, TILES], F32, name="rms")
+        def root(n, first=0, tiles=TILES):
+            if first == 0:
+                rms_of[n] = stat_pool.tile([P, TILES], F32, name="rms")
             nc.scalar.activation(
-                out=rms[:], in_=sum_sq_of[n][:], func=ACT.Sqrt, scale=1.0 / E, bias=EPS
+                out=rms_of[n][:, first : first + tiles],
+                in_=sum_sq_of[n][:, first : first + tiles],
+                func=ACT.Sqrt,
+                scale=1.0 / E,
+                bias=EPS,
             )
-            rms_of[n] = rms
 
-        def invert(n):
-            rstd = stat_pool.tile([P, TILES], F32, name="rstd")
-            nc.vector.reciprocal(rstd[:], rms_of[n][:])
-            rstd_of[n] = rstd
+        def invert(n, first=0, tiles=TILES):
+            if first == 0:
+                rstd_of[n] = stat_pool.tile([P, TILES], F32, name="rstd")
+            nc.vector.reciprocal(
+                rstd_of[n][:, first : first + tiles], rms_of[n][:, first : first + tiles]
+            )
 
         def gpsimd_scale(n):
             scaled = work.tile([P, GPSIMD_COLS], F32, name="scaled")
@@ -192,60 +199,60 @@ def tile_block_pa_t_kernel(tc, x, scale1, w_qkv, out_0, out_1, out_2):
             )
             scaled_of[n] = scaled
 
-        def normalise_and_turn(n):
-            xn = work.tile([P, TILES, E], BF16, name="xn")
-            xn_words = xn[:].bitcast(F32)
+        def gpsimd_normalise(n):
             for j in range(TILES):
-                first = vector_share(j)
+                first = vector_share(n, j)
                 if first < E:
                     start = j * E + first - VECTOR_COLS
                     nc.gpsimd.tensor_scalar(
-                        out=xn[:, j, first:],
+                        out=xn_of[n][:, j, first:],
                         in0=scaled_of[n][:, start : start + E - first],
                         scalar1=rstd_of[n][:, j : j + 1],
                         scalar2=0.0,
                         op0=ALU.mult,
                         op1=ALU.add,
                     )
-            turned_of[n] = []
-            for j in range(TILES):
-                share = vector_share(j)
-                if share > 0:
-                    nc.vector.scalar_tensor_tensor(
-                        out=xn[:, j, :share],
-                        in0=x_tiles[n][:, j, :share],
-                        scalar=rstd_of[n][:, j : j + 1],
-                        in1=gain_bank[:, :share],
-                        op0=ALU.mult,
-                        op1=ALU.mult,
-                    )
-                turned = turned_psum.tile([P, BLOCKS, P], F32, name="turned")
-                for b in range(BLOCKS):
-                    nc.tensor.transpose(
-                        turned[:, b, :], xn_words[:, j, b * P : (b + 1) * P], ident[:]
-                    )
-                turned_of[n].append(turned)
+
+        def vector_normalise(n, j):
+            share = vector_share(n, j)
+            if share > 0:
+                nc.vector.scalar_tensor_tensor(
+                    out=xn_of[n][:, j, :share],
+                    in0=x_tiles[n][:, j, :share],
+                    scalar=rstd_of[n][:, j : j + 1],
+                    in1=gain_bank[:, :share],
+                    op0=ALU.mult,
+                    op1=ALU.mult,
+                )
+
+        def turn(n, j):
+            turned = turned_psum.tile([P, BLOCKS, P], F32, name="turned")
+            words = xn_of[n][:].bitcast(F32)
+            for b in range(BLOCKS):
+                nc.tensor.transpose(turned[:, b, :], words[:, j, b * P : (b + 1) * P], ident[:])
+            turned_of[n, j] = turned
+
+        def start_group(n):
+            xn_of[n] = work.tile([P, TILES, E], BF16, name="xn")
             grouped_of[n] = work.tile(
                 [P, TILES, PASSES, P, PACK], BF16, align_bytes=64, name="grouped"
             )
+            codes_of[n] = work.tile([P, TILES, PASSES, P], U32, align_bytes=64, name="codes")
+            scales_of[n] = work.tile([P, TILES, PASSES, P], U8, align_bytes=64, name="scales")
 
-        def copy_turned(n, j):
-            copy = nc.vector.tensor_copy if j == VECTOR_BANK or n < SUMS_LAG else nc.scalar.copy
+        def copy_turned(n, j, copy):
             copy(
                 out=grouped_of[n][:].bitcast(F32)[:, j],
-                in_=turned_of[n][j][:].rearrange("p (g u) r -> p g r u", u=2),
+                in_=turned_of[n, j][:].rearrange("p (g u) r -> p g r u", u=2),
             )
 
-        def quantise(n):
-            codes = work.tile([P, TILES, PASSES, P], U32, align_bytes=64, name="codes")
-            scales = work.tile([P, TILES, PASSES, P], U8, align_bytes=64, name="scales")
+        def quantise(n, first=0, tiles=TILES):
+            last = first + tiles
             nc.vector.quantize_mx(
-                out=codes[:].rearrange("p j g r -> p (j g r)").bitcast(FP8X4),
-                scales=scales[:].rearrange("p j g r -> p (j g r)"),
-                in_=grouped_of[n][:].rearrange("p j g r t -> p (j g r t)"),
+                out=codes_of[n][:, first:last].rearrange("p j g r -> p (j g r)").bitcast(FP8X4),
+                scales=scales_of[n][:, first:last].rearrange("p j g r -> p (j g r)"),
+                in_=grouped_of[n][:, first:last].rearrange("p j g r t -> p (j g r t)"),
             )
-            codes_of[n] = codes
-            scales_of[n] = scales
 
         def multiply(n, j, c0, c1, out):
             for g in range(PASSES):
@@ -271,10 +278,17 @@ def tile_block_pa_t_kernel(tc, x, scale1, w_qkv, out_0, out_1, out_2):
                 multiply(n, j, QK_COLS, COLS, v_bank[:, j, :])
             acc_of[n] = (qk_banks, v_bank)
 
-        def copy_and_store(n):
-            copy = nc.vector.tensor_copy if in_range(n + SUMS_LAG + 2) else nc.scalar.copy
+        def store(n, s, first=0, tiles=TILES):
+            c0, c1 = first * PART_COLS, (first + tiles) * PART_COLS
+            nc.sync.dma_start(
+                out=out_groups[s][n][:, c0:c1],
+                in_=result_of[n][:, s, first : first + tiles].rearrange("p j c -> p (j c)"),
+            )
+
+        def copy_and_store(n, copy):
             qk_banks, v_bank = acc_of[n]
             result = out_pool.tile([P, PARTS, TILES, PART_COLS], F32, name="result")
+            result_of[n] = result
             for i, qk in enumerate(qk_banks):
                 copy(
                     out=result[:, 0:2, 2 * i : 2 * i + 2, :],
@@ -282,41 +296,70 @@ def tile_block_pa_t_kernel(tc, x, scale1, w_qkv, out_0, out_1, out_2):
                 )
             copy(out=result[:, 2], in_=v_bank[:])
             for s in range(PARTS):
-                nc.sync.dma_start(
-                    out=out_groups[s][n], in_=result[:, s].rearrange("p j c -> p (j c)")
-                )
+                store(n, s)
 
-        sum_squares(0)
-        root(0)
-        sum_squares(1)
-        regroup_weights(0)
+        def project_tile(n, j):
+            acc = turned_psum.tile([P, COLS], F32, name="turned")
+            for c0, c1 in COLUMN_CUTS:
+                multiply(n, j, c0, c1, acc[:, c0:c1])
+            acc_of[n, j] = acc
+
+        def copy_tile(n, j, copy):
+            copy(
+                out=result_of[n][:, :, j, :],
+                in_=acc_of[n, j][:].rearrange("p (s c) -> p s c", s=PARTS),
+            )
+
+        for n in (0, 1):
+            sum_sq_of[n] = stat_pool.tile([P, TILES], F32, name="sum_sq")
         spread_gain()
-        regroup_weights(1)
-        quantise_weights()
-        invert(0)
-        gpsimd_scale(0)
+        for j in range(TILES):
+            square_tile(0, j)
+            if j > 0:
+                root(0, j - 1, 1)
+        square_tile(1, 0)
+        root(0, TILES - 1, 1)
+        for j in range(1, TILES):
+            square_tile(1, j)
 
+        vec, sca = nc.vector.tensor_copy, nc.scalar.copy
         for r in range(GROUPS + SUMS_LAG):
-            if in_range(r - 1):
-                copy_turned(r - 1, VECTOR_BANK)
             if in_range(r):
-                normalise_and_turn(r)
-                copy_turned(r, 0)
+                start_group(r)
+                if r > 1:
+                    copy_turned(r - 1, VECTOR_BANK, vec)
+                if r > 0:
+                    gpsimd_normalise(r)
+                for j in range(TILES):
+                    if r == 0:
+                        invert(0, j, 1)
+                    vector_normalise(r, j)
+                    if r == 1:
+                        copy_turned(0, j, vec)
+                    turn(r, j)
+                if r > 0:
+                    copy_turned(r, 0, sca)
+                if r == 0:
+                    regroup_weights(0)
+                    regroup_weights(1)
+                    quantise_weights()
+            elif in_range(r - 1):
+                copy_turned(r - 1, VECTOR_BANK, vec)
             if in_range(r + 1):
                 root(r + 1)
+            if in_range(r - SUMS_LAG):
+                copy_and_store(r - SUMS_LAG, vec if r - SUMS_LAG < 12 else sca)
             if in_range(r - 1):
                 quantise(r - 1)
             if in_range(r + 1):
                 invert(r + 1)
                 gpsimd_scale(r + 1)
-            if in_range(r + 2):
+            if r + 2 < GROUPS:
                 sum_sq_of[r + 2] = stat_pool.tile([P, TILES], F32, name="sum_sq")
             for j in range(TILES):
-                if in_range(r) and 1 <= j < VECTOR_BANK:
-                    copy_turned(r, j)
+                if 0 < r < GROUPS and 1 <= j < VECTOR_BANK:
+                    copy_turned(r, j, sca)
                 if in_range(r + 2):
                     square_tile(r + 2, j)
-            if in_range(r - SUMS_LAG):
-                copy_and_store(r - SUMS_LAG)
             if in_range(r - 1):
                 project(r - 1)

@@ -28,22 +28,25 @@ BLOCKS = WORDS // P
 TILES = 4
 GROUP_ROWS = P * TILES
 GROUPS = ROWS // GROUP_ROWS
+LAST = GROUPS - 1
 
 PART_COLS = HEADS * D
 QK_COLS = 2 * PART_COLS
 COLUMN_CUTS = ((0, QK_COLS), (QK_COLS, COLS))
 BANK = 512
+BANKS = 3
 
-GPSIMD_COLS = E + E // 4
-VECTOR_COLS = TILES * E - GPSIMD_COLS
-VECTOR_BANK = TILES - 1
-SUMS_LAG = 2
+GPSIMD_MAX = 1280
 
 FLOPS = 2 * ROWS * E * COLS
 
 
+def gpsimd_cols(n):
+    return (E * 3 // 4 if n in (1, LAST) else E * 5 // 4) if n else 0
+
+
 def vector_share(n, j):
-    return E if n == 0 else min(E, max(0, VECTOR_COLS - j * E))
+    return min(E, max(0, TILES * E - gpsimd_cols(n) - j * E))
 
 
 def tile_block_pa_t_kernel(tc, x, scale1, w_qkv, out_0, out_1, out_2):
@@ -63,13 +66,14 @@ def tile_block_pa_t_kernel(tc, x, scale1, w_qkv, out_0, out_1, out_2):
         const = ctx.enter_context(tc.tile_pool(name="const", bufs=1))
         x_pool = ctx.enter_context(tc.tile_pool(name="x_pool", bufs=GROUPS))
         stat_pool = ctx.enter_context(tc.tile_pool(name="stat_pool", bufs=4))
-        square_pool = ctx.enter_context(tc.tile_pool(name="square_pool", bufs=4))
+        square_pool = ctx.enter_context(tc.tile_pool(name="square_pool", bufs=2))
         work = ctx.enter_context(tc.tile_pool(name="work", bufs=2))
         out_pool = ctx.enter_context(tc.tile_pool(name="out_pool", bufs=3))
         gain_psum = ctx.enter_context(tc.psum_pool(name="gain_psum", bufs=1))
         turned_psum = ctx.enter_context(tc.psum_pool(name="turned_psum", bufs=TILES))
-        acc_psum = ctx.enter_context(tc.psum_pool(name="acc_psum", bufs=3))
+        acc_psum = ctx.enter_context(tc.psum_pool(name="acc_psum", bufs=BANKS))
         ctx.enter_context(tc.manual_schedule())
+        vec, sca = nc.vector.tensor_copy, nc.scalar.copy
 
         x_tiles = [x_pool.tile([P, TILES, E], BF16, name="x_sb") for n in range(GROUPS)]
 
@@ -96,10 +100,11 @@ def tile_block_pa_t_kernel(tc, x, scale1, w_qkv, out_0, out_1, out_2):
         nc.sync.dma_start(out=gain_row[0:1, :], in_=scale1.unsqueeze(0))
         for j in range(1, TILES):
             load_x(0, j, 1)
-        load_x(1, 0, 2)
-        load_x(1, 2, 2)
         load_w(0)
+        load_x(1, 0, 1)
         load_w(1)
+        load_x(1, 1, 1)
+        load_x(1, 2, 2)
         for n in range(2, GROUPS):
             load_x(n, 0, TILES)
 
@@ -112,35 +117,39 @@ def tile_block_pa_t_kernel(tc, x, scale1, w_qkv, out_0, out_1, out_2):
         nc.scalar.activation(out=warm[:], in_=warm[:], func=ACT.Sqrt)
 
         gain_bank = gain_psum.tile([P, E], BF16)
-        gpsimd_gain = const.tile([P, GPSIMD_COLS], BF16)
-
-        def spread_gain():
-            for c0 in range(0, E, BANK):
-                nc.tensor.matmul(
-                    out=gain_bank[:, c0 : c0 + BANK],
-                    lhsT=ones[:],
-                    rhs=gain_row[:, c0 : c0 + BANK],
-                    start=True,
-                    stop=True,
-                )
-            nc.vector.tensor_copy(
-                out=gpsimd_gain[:, : GPSIMD_COLS - E], in_=gain_bank[:, 2 * E - GPSIMD_COLS :]
+        for c0 in range(0, E, BANK):
+            nc.tensor.matmul(
+                out=gain_bank[:, c0 : c0 + BANK],
+                lhsT=ones[:],
+                rhs=gain_row[:, c0 : c0 + BANK],
+                start=True,
+                stop=True,
             )
-            nc.vector.tensor_copy(out=gpsimd_gain[:, GPSIMD_COLS - E :], in_=gain_bank[:])
+
+        gpsimd_gain = const.tile([P, GPSIMD_MAX], BF16)
+
+        def gain_for_gpsimd():
+            nc.vector.tensor_copy(
+                out=gpsimd_gain[:, : GPSIMD_MAX - E], in_=gain_bank[:, 2 * E - GPSIMD_MAX :]
+            )
+            nc.vector.tensor_copy(out=gpsimd_gain[:, GPSIMD_MAX - E :], in_=gain_bank[:])
 
         w_grouped = const.tile([P, PASSES, COLS, PACK], BF16, align_bytes=64)
         w_codes = const.tile([P, PASSES, COLS], U32, align_bytes=64)
         w_scales = const.tile([P, PASSES, COLS], U8, align_bytes=64)
 
-        def regroup_weights(g):
+        def regroup_weights(g, on_gpsimd):
             by_part = w_raw[:, g].rearrange("p t (h s d) -> p s h d t", h=HEADS, s=PARTS)
             for s in range(PARTS):
-                nc.vector.tensor_copy(
-                    out=w_grouped[:, g, s * PART_COLS : (s + 1) * PART_COLS, :].rearrange(
-                        "p (h d) t -> p h d t", h=HEADS
-                    ),
-                    in_=by_part[:, s],
+                out = w_grouped[:, g, s * PART_COLS : (s + 1) * PART_COLS, :].rearrange(
+                    "p (h d) t -> p h d t", h=HEADS
                 )
+                if on_gpsimd:
+                    nc.gpsimd.tensor_scalar(
+                        out=out, in0=by_part[:, s], scalar1=1.0, scalar2=0.0, op0=ALU.mult, op1=ALU.add
+                    )
+                else:
+                    nc.vector.tensor_copy(out=out, in_=by_part[:, s])
 
         def quantise_weights():
             for g in range(PASSES):
@@ -151,11 +160,14 @@ def tile_block_pa_t_kernel(tc, x, scale1, w_qkv, out_0, out_1, out_2):
                         in_=w_grouped[:, g, c0:c1, :].rearrange("p c t -> p (c t)"),
                     )
 
-        sum_sq_of, rms_of, rstd_of, scaled_of, turned_of = {}, {}, {}, {}, {}
-        grouped_of, codes_of, scales_of, acc_of, xn_of, result_of = {}, {}, {}, {}, {}, {}
+        sum_sq_of, rms_of, rstd_of, xn_of, turned_of = {}, {}, {}, {}, {}
+        grouped_of, codes_of, scales_of, acc_of, result_of = {}, {}, {}, {}, {}
+        scaled_of = {}
 
-        def in_range(n):
-            return 0 <= n < GROUPS
+        def start_statistics(n):
+            sum_sq_of[n] = stat_pool.tile([P, TILES], F32, name="sum_sq")
+            rms_of[n] = stat_pool.tile([P, TILES], F32, name="rms")
+            rstd_of[n] = stat_pool.tile([P, TILES], F32, name="rstd")
 
         def square_tile(n, j):
             squares = square_pool.tile([P, E], BF16, name="squares")
@@ -166,44 +178,35 @@ def tile_block_pa_t_kernel(tc, x, scale1, w_qkv, out_0, out_1, out_2):
                 accum_out=sum_sq_of[n][:, j : j + 1],
             )
 
-        def sum_squares(n):
-            sum_sq_of[n] = stat_pool.tile([P, TILES], F32, name="sum_sq")
-            for j in range(TILES):
-                square_tile(n, j)
-
-        def root(n, first=0, tiles=TILES):
-            if first == 0:
-                rms_of[n] = stat_pool.tile([P, TILES], F32, name="rms")
-            nc.scalar.activation(
-                out=rms_of[n][:, first : first + tiles],
-                in_=sum_sq_of[n][:, first : first + tiles],
-                func=ACT.Sqrt,
-                scale=1.0 / E,
-                bias=EPS,
-            )
-
-        def invert(n, first=0, tiles=TILES):
-            if first == 0:
-                rstd_of[n] = stat_pool.tile([P, TILES], F32, name="rstd")
-            nc.vector.reciprocal(
-                rstd_of[n][:, first : first + tiles], rms_of[n][:, first : first + tiles]
+        def vector_square(n, j):
+            squares = const.tile([P, E], F32, name="vector_squares")
+            nc.vector.scalar_tensor_tensor(
+                out=squares[:],
+                in0=x_tiles[n][:, j, :],
+                scalar=1.0,
+                in1=x_tiles[n][:, j, :],
+                op0=ALU.mult,
+                op1=ALU.mult,
+                accum_out=sum_sq_of[n][:, j : j + 1],
             )
 
         def gpsimd_scale(n):
-            scaled = work.tile([P, GPSIMD_COLS], F32, name="scaled")
+            cols = gpsimd_cols(n)
+            scaled = work.tile([P, GPSIMD_MAX], F32, name="scaled")
             nc.gpsimd.tensor_tensor(
-                out=scaled[:],
-                in0=x_tiles[n][:].rearrange("p j e -> p (j e)")[:, VECTOR_COLS:],
-                in1=gpsimd_gain[:],
+                out=scaled[:, :cols],
+                in0=x_tiles[n][:].rearrange("p j e -> p (j e)")[:, TILES * E - cols :],
+                in1=gpsimd_gain[:, GPSIMD_MAX - cols :],
                 op=ALU.mult,
             )
             scaled_of[n] = scaled
 
         def gpsimd_normalise(n):
+            cols = gpsimd_cols(n)
             for j in range(TILES):
                 first = vector_share(n, j)
                 if first < E:
-                    start = j * E + first - VECTOR_COLS
+                    start = j * E + first - (TILES * E - cols)
                     nc.gpsimd.tensor_scalar(
                         out=xn_of[n][:, j, first:],
                         in0=scaled_of[n][:, start : start + E - first],
@@ -213,7 +216,27 @@ def tile_block_pa_t_kernel(tc, x, scale1, w_qkv, out_0, out_1, out_2):
                         op1=ALU.add,
                     )
 
-        def vector_normalise(n, j):
+        def root(n, first, tiles):
+            nc.scalar.activation(
+                out=rms_of[n][:, first : first + tiles],
+                in_=sum_sq_of[n][:, first : first + tiles],
+                func=ACT.Sqrt,
+                scale=1.0 / E,
+                bias=EPS,
+            )
+
+        def invert(n, first=0, tiles=TILES):
+            nc.vector.reciprocal(
+                rstd_of[n][:, first : first + tiles], rms_of[n][:, first : first + tiles]
+            )
+
+        def start_group(n):
+            xn_of[n] = work.tile([P, TILES, E], BF16, name="xn")
+            grouped_of[n] = work.tile(
+                [P, TILES, PASSES, P, PACK], BF16, align_bytes=64, name="grouped"
+            )
+
+        def normalise(n, j):
             share = vector_share(n, j)
             if share > 0:
                 nc.vector.scalar_tensor_tensor(
@@ -232,14 +255,6 @@ def tile_block_pa_t_kernel(tc, x, scale1, w_qkv, out_0, out_1, out_2):
                 nc.tensor.transpose(turned[:, b, :], words[:, j, b * P : (b + 1) * P], ident[:])
             turned_of[n, j] = turned
 
-        def start_group(n):
-            xn_of[n] = work.tile([P, TILES, E], BF16, name="xn")
-            grouped_of[n] = work.tile(
-                [P, TILES, PASSES, P, PACK], BF16, align_bytes=64, name="grouped"
-            )
-            codes_of[n] = work.tile([P, TILES, PASSES, P], U32, align_bytes=64, name="codes")
-            scales_of[n] = work.tile([P, TILES, PASSES, P], U8, align_bytes=64, name="scales")
-
         def copy_turned(n, j, copy):
             copy(
                 out=grouped_of[n][:].bitcast(F32)[:, j],
@@ -247,6 +262,9 @@ def tile_block_pa_t_kernel(tc, x, scale1, w_qkv, out_0, out_1, out_2):
             )
 
         def quantise(n, first=0, tiles=TILES):
+            if first == 0:
+                codes_of[n] = work.tile([P, TILES, PASSES, P], U32, align_bytes=64, name="codes")
+                scales_of[n] = work.tile([P, TILES, PASSES, P], U8, align_bytes=64, name="scales")
             last = first + tiles
             nc.vector.quantize_mx(
                 out=codes_of[n][:, first:last].rearrange("p j g r -> p (j g r)").bitcast(FP8X4),
@@ -266,100 +284,155 @@ def tile_block_pa_t_kernel(tc, x, scale1, w_qkv, out_0, out_1, out_2):
                     stop=(g == PASSES - 1),
                 )
 
-        def project(n):
-            qk_banks = []
-            for first in range(0, TILES, 2):
-                qk = acc_psum.tile([P, 2, QK_COLS], F32, name="acc")
+        def project(n, bank):
+            if bank < 2:
+                acc = acc_psum.tile([P, 2, QK_COLS], F32, name="acc")
                 for i in range(2):
-                    multiply(n, first + i, 0, QK_COLS, qk[:, i, :])
-                qk_banks.append(qk)
-            v_bank = acc_psum.tile([P, TILES, PART_COLS], F32, name="acc")
-            for j in range(TILES):
-                multiply(n, j, QK_COLS, COLS, v_bank[:, j, :])
-            acc_of[n] = (qk_banks, v_bank)
+                    multiply(n, 2 * bank + i, 0, QK_COLS, acc[:, i, :])
+            else:
+                acc = acc_psum.tile([P, TILES, PART_COLS], F32, name="acc")
+                for j in range(TILES):
+                    multiply(n, j, QK_COLS, COLS, acc[:, j, :])
+            acc_of[n, bank] = acc
 
-        def store(n, s, first=0, tiles=TILES):
-            c0, c1 = first * PART_COLS, (first + tiles) * PART_COLS
-            nc.sync.dma_start(
-                out=out_groups[s][n][:, c0:c1],
-                in_=result_of[n][:, s, first : first + tiles].rearrange("p j c -> p (j c)"),
-            )
+        def start_result(n):
+            result_of[n] = out_pool.tile([P, PARTS, TILES, PART_COLS], F32, name="result")
 
-        def copy_and_store(n, copy):
-            qk_banks, v_bank = acc_of[n]
-            result = out_pool.tile([P, PARTS, TILES, PART_COLS], F32, name="result")
-            result_of[n] = result
-            for i, qk in enumerate(qk_banks):
+        def copy_bank(n, bank, copy):
+            if bank < 2:
                 copy(
-                    out=result[:, 0:2, 2 * i : 2 * i + 2, :],
-                    in_=qk[:].rearrange("p j (s c) -> p s j c", s=2),
+                    out=result_of[n][:, 0:2, 2 * bank : 2 * bank + 2, :],
+                    in_=acc_of[n, bank][:].rearrange("p j (s c) -> p s j c", s=2),
                 )
-            copy(out=result[:, 2], in_=v_bank[:])
+            else:
+                copy(out=result_of[n][:, 2], in_=acc_of[n, bank][:])
+
+        def store(n, first=0, tiles=TILES):
+            c0, c1 = first * PART_COLS, (first + tiles) * PART_COLS
             for s in range(PARTS):
-                store(n, s)
+                nc.sync.dma_start(
+                    out=out_groups[s][n][:, c0:c1],
+                    in_=result_of[n][:, s, first : first + tiles].rearrange("p j c -> p (j c)"),
+                )
 
         def project_tile(n, j):
             acc = turned_psum.tile([P, COLS], F32, name="turned")
             for c0, c1 in COLUMN_CUTS:
                 multiply(n, j, c0, c1, acc[:, c0:c1])
-            acc_of[n, j] = acc
+            acc_of[n, "tile", j] = acc
 
         def copy_tile(n, j, copy):
             copy(
                 out=result_of[n][:, :, j, :],
-                in_=acc_of[n, j][:].rearrange("p (s c) -> p s c", s=PARTS),
+                in_=acc_of[n, "tile", j][:].rearrange("p (s c) -> p s c", s=PARTS),
             )
 
+        VB = TILES - 1
         for n in (0, 1):
-            sum_sq_of[n] = stat_pool.tile([P, TILES], F32, name="sum_sq")
-        spread_gain()
-        for j in range(TILES):
+            start_statistics(n)
+        vector_square(0, 1)
+        order = (0, 2, 3)
+        done = [1]
+        for j in order:
             square_tile(0, j)
-            if j > 0:
-                root(0, j - 1, 1)
+            root(0, {0: 0, 2: 1, 3: 2}[j], 1)
         square_tile(1, 0)
-        root(0, TILES - 1, 1)
+        root(0, 3, 1)
         for j in range(1, TILES):
             square_tile(1, j)
-
-        vec, sca = nc.vector.tensor_copy, nc.scalar.copy
-        for r in range(GROUPS + SUMS_LAG):
-            if in_range(r):
-                start_group(r)
-                if r > 1:
-                    copy_turned(r - 1, VECTOR_BANK, vec)
-                if r > 0:
-                    gpsimd_normalise(r)
-                for j in range(TILES):
-                    if r == 0:
-                        invert(0, j, 1)
-                    vector_normalise(r, j)
-                    if r == 1:
-                        copy_turned(0, j, vec)
-                    turn(r, j)
-                if r > 0:
-                    copy_turned(r, 0, sca)
-                if r == 0:
-                    regroup_weights(0)
-                    regroup_weights(1)
-                    quantise_weights()
-            elif in_range(r - 1):
-                copy_turned(r - 1, VECTOR_BANK, vec)
-            if in_range(r + 1):
-                root(r + 1)
-            if in_range(r - SUMS_LAG):
-                copy_and_store(r - SUMS_LAG, vec if r - SUMS_LAG < 12 else sca)
-            if in_range(r - 1):
-                quantise(r - 1)
-            if in_range(r + 1):
-                invert(r + 1)
-                gpsimd_scale(r + 1)
-            if r + 2 < GROUPS:
-                sum_sq_of[r + 2] = stat_pool.tile([P, TILES], F32, name="sum_sq")
+        root(1, 0, TILES)
+        start_group(0)
+        for j in range(TILES):
+            invert(0, j, 1)
+            normalise(0, j)
+            turn(0, j)
+            if j == 9:
+                gain_for_gpsimd()
+        regroup_weights(0, True)
+        regroup_weights(1, True)
+        quantise_weights()
+        gain_for_gpsimd()
+        invert(1)
+        gpsimd_scale(1)
+        start_statistics(2)
+        for j in range(TILES):
+            square_tile(2, j)
+        for r in range(1, LAST):
+            old = r >= 2
+            start_group(r)
+            if old:
+                start_result(r - 2)
+            if r > 1:
+                copy_turned(r - 1, VB, vec)
+            gpsimd_normalise(r)
             for j in range(TILES):
-                if 0 < r < GROUPS and 1 <= j < VECTOR_BANK:
+                normalise(r, j)
+                if r == 1:
+                    copy_turned(0, j, vec)
+                turn(r, j)
+                if old and j == 0:
+                    project(r - 2, 2)
+            copy_turned(r, 0, sca)
+            root(r + 1, 0, TILES)
+            if old:
+                for bank in range(BANKS):
+                    copy_bank(r - 2, bank, vec if r < LAST - 1 else sca)
+                store(r - 2)
+            quantise(r - 1)
+            invert(r + 1)
+            gpsimd_scale(r + 1)
+            if r + 2 < GROUPS:
+                start_statistics(r + 2)
+            for j in range(TILES):
+                if 1 <= j < VB:
                     copy_turned(r, j, sca)
-                if in_range(r + 2):
+                if r + 2 < GROUPS:
                     square_tile(r + 2, j)
-            if in_range(r - 1):
-                project(r - 1)
+            project(r - 1, 0)
+            project(r - 1, 1)
+        n = LAST
+        start_group(n)
+        start_result(n - 2)
+        gpsimd_normalise(n)
+        copy_turned(n - 1, VB, sca)
+        normalise(n, 0)
+        turn(n, 0)
+        project(n - 2, 2)
+        copy_turned(n, 0, sca)
+        normalise(n, 1)
+        turn(n, 1)
+        copy_bank(n - 2, 0, sca)
+        copy_turned(n, 1, sca)
+        quantise(n - 1)
+        copy_bank(n - 2, 1, sca)
+        normalise(n, 3)
+        turn(n, 3)
+        start_result(n - 1)
+        project(n - 1, 0)
+        copy_turned(n, 3, sca)
+        copy_bank(n - 2, 2, sca)
+        store(n - 2)
+        normalise(n, 2)
+        turn(n, 2)
+        project(n - 1, 1)
+        copy_turned(n, 2, sca)
+        quantise(n, 0, 1)
+        project_tile(n, 0)
+        quantise(n, 1, 1)
+        project_tile(n, 1)
+        copy_bank(n - 1, 0, vec)
+        project(n - 1, 2)
+        quantise(n, 3, 1)
+        project_tile(n, 3)
+        quantise(n, 2, 1)
+        copy_bank(n - 1, 1, sca)
+        copy_bank(n - 1, 2, sca)
+        store(n - 1)
+        start_result(n)
+        project_tile(n, 2)
+        copy_tile(n, 0, vec)
+        copy_tile(n, 1, sca)
+        store(n, 0, 2)
+        copy_tile(n, 3, vec)
+        copy_tile(n, 2, sca)
+        store(n, 2, 2)

@@ -36,13 +36,13 @@ COLUMN_CUTS = ((0, QK_COLS), (QK_COLS, COLS))
 BANK = 512
 BANKS = 3
 
-GPSIMD_MAX = 1280
+GPSIMD_MAX = 1344
 
 FLOPS = 2 * ROWS * E * COLS
 
 
 def gpsimd_cols(n):
-    return (E * 3 // 4 if n in (1, LAST) else E * 5 // 4) if n else 0
+    return (E * 3 // 4 if n in (1, LAST) else E * 21 // 16) if n else 0
 
 
 def vector_share(n, j):
@@ -98,9 +98,10 @@ def tile_block_pa_t_kernel(tc, x, scale1, w_qkv, out_0, out_1, out_2):
 
         load_x(0, 0, 1)
         nc.sync.dma_start(out=gain_row[0:1, :], in_=scale1.unsqueeze(0))
-        for j in range(1, TILES):
-            load_x(0, j, 1)
+        load_x(0, 1, 1)
+        load_x(0, 2, 1)
         load_w(0)
+        load_x(0, 3, 1)
         load_x(1, 0, 1)
         load_w(1)
         load_x(1, 1, 1)

@@ -36,13 +36,13 @@ COLUMN_CUTS = ((0, QK_COLS), (QK_COLS, COLS))
 BANK = 512
 BANKS = 3
 
-GPSIMD_MAX = 1344
+GPSIMD_MAX = 1280
 
 FLOPS = 2 * ROWS * E * COLS
 
 
 def gpsimd_cols(n):
-    return (E * 3 // 4 if n in (1, LAST) else E * 21 // 16) if n else 0
+    return (E * 3 // 4 if n in (1, LAST) else E * 5 // 4) if n else 0
 
 
 def vector_share(n, j):
@@ -399,13 +399,13 @@ def tile_block_pa_t_kernel(tc, x, scale1, w_qkv, out_0, out_1, out_2):
         normalise(n, 0)
         turn(n, 0)
         project(n - 2, 2)
+        copy_bank(n - 2, 0, sca)
+        copy_bank(n - 2, 1, sca)
         copy_turned(n, 0, sca)
         normalise(n, 1)
         turn(n, 1)
-        copy_bank(n - 2, 0, sca)
         copy_turned(n, 1, sca)
         quantise(n - 1)
-        copy_bank(n - 2, 1, sca)
         normalise(n, 3)
         turn(n, 3)
         start_result(n - 1)
@@ -416,13 +416,13 @@ def tile_block_pa_t_kernel(tc, x, scale1, w_qkv, out_0, out_1, out_2):
         normalise(n, 2)
         turn(n, 2)
         project(n - 1, 1)
+        project(n - 1, 2)
         copy_turned(n, 2, sca)
         quantise(n, 0, 1)
         project_tile(n, 0)
         quantise(n, 1, 1)
         project_tile(n, 1)
         copy_bank(n - 1, 0, vec)
-        project(n - 1, 2)
         quantise(n, 3, 1)
         project_tile(n, 3)
         quantise(n, 2, 1)

@@ -42,7 +42,7 @@ FLOPS = 2 * ROWS * E * COLS
 
 
 def gpsimd_cols(n):
-    return (E * 3 // 4 if n in (1, LAST) else E * 5 // 4) if n else 0
+    return (E * 5 // 8 if n in (1, LAST) else E * 5 // 4) if n else 0
 
 
 def vector_share(n, j):

from contextlib import ExitStack

import concourse.mybir as mybir
from concourse.masks import make_identity

F32 = mybir.dt.float32
BF16 = mybir.dt.bfloat16
U32 = mybir.dt.uint32
U8 = mybir.dt.uint8
FP8X4 = mybir.dt.float8_e4m3fn_x4
ACT = mybir.ActivationFunctionType
ALU = mybir.AluOpType

P = 128
ROWS = 4 * 2048
E = 1024
HEADS = 2
PARTS = 3
D = 64
COLS = HEADS * PARTS * D
EPS = 1e-6

PACK = 4
PASSES = E // (P * PACK)
WORDS = E // 2
BLOCKS = WORDS // P

TILES = 4
GROUP_ROWS = P * TILES
GROUPS = ROWS // GROUP_ROWS
LAST = GROUPS - 1

PART_COLS = HEADS * D
QK_COLS = 2 * PART_COLS
COLUMN_CUTS = ((0, QK_COLS), (QK_COLS, COLS))
BANK = 512
BANKS = 3

GPSIMD_MAX = 1280

FLOPS = 2 * ROWS * E * COLS


def gpsimd_cols(n):
    return (E * 5 // 8 if n in (1, LAST) else E * 5 // 4) if n else 0


def vector_share(n, j):
    return min(E, max(0, TILES * E - gpsimd_cols(n) - j * E))


def tile_block_pa_t_kernel(tc, x, scale1, w_qkv, out_0, out_1, out_2):
    nc = tc.nc

    x_groups = x.rearrange("b s e -> (b s) e").rearrange(
        "(n p j) e -> n p (j e)", p=P, j=TILES
    )
    out_groups = [
        out.rearrange("b s h d -> (b s) (h d)").rearrange(
            "(n p j) c -> n p (j c)", p=P, j=TILES
        )
        for out in (out_0, out_1, out_2)
    ]

    with ExitStack() as ctx:
        const = ctx.enter_context(tc.tile_pool(name="const", bufs=1))
        x_pool = ctx.enter_context(tc.tile_pool(name="x_pool", bufs=GROUPS))
        stat_pool = ctx.enter_context(tc.tile_pool(name="stat_pool", bufs=4))
        square_pool = ctx.enter_context(tc.tile_pool(name="square_pool", bufs=2))
        work = ctx.enter_context(tc.tile_pool(name="work", bufs=2))
        out_pool = ctx.enter_context(tc.tile_pool(name="out_pool", bufs=3))
        gain_psum = ctx.enter_context(tc.psum_pool(name="gain_psum", bufs=1))
        turned_psum = ctx.enter_context(tc.psum_pool(name="turned_psum", bufs=TILES))
        acc_psum = ctx.enter_context(tc.psum_pool(name="acc_psum", bufs=BANKS))
        ctx.enter_context(tc.manual_schedule())
        vec, sca = nc.vector.tensor_copy, nc.scalar.copy

        x_tiles = [x_pool.tile([P, TILES, E], BF16, name="x_sb") for n in range(GROUPS)]

        def load_x(n, first_tile, tiles):
            c0, c1 = first_tile * E, (first_tile + tiles) * E
            nc.sync.dma_start(
                out=x_tiles[n][:].rearrange("p j e -> p (j e)")[:, c0:c1], in_=x_groups[n][:, c0:c1]
            )

        w_raw = const.tile([P, PASSES, PACK, COLS], BF16)
        w_passes = w_qkv.rearrange("k h c -> k (h c)").rearrange(
            "(g u p e) c -> g p u (e c)", g=PASSES, p=P, e=2
        )

        def load_w(g):
            nc.sync.dma_start(
                out=w_raw[:, g].rearrange("p (u e) c -> p u (e c)", e=2), in_=w_passes[g]
            )

        gain_row = const.tile([P, E], BF16)
        nc.vector.memset(gain_row[:], 0.0)

        load_x(0, 0, 1)
        nc.sync.dma_start(out=gain_row[0:1, :], in_=scale1.unsqueeze(0))
        load_x(0, 1, 1)
        load_x(0, 2, 1)
        load_w(0)
        load_x(0, 3, 1)
        load_x(1, 0, 1)
        load_w(1)
        load_x(1, 1, 1)
        load_x(1, 2, 2)
        for n in range(2, GROUPS):
            load_x(n, 0, TILES)

        ident = const.tile([P, P], F32)
        make_identity(nc, ident[:])
        ones = const.tile([P, P], BF16)
        nc.vector.memset(ones[:], 1.0)
        warm = const.tile([P, 1], F32)
        nc.vector.memset(warm[:], 1.0)
        nc.scalar.activation(out=warm[:], in_=warm[:], func=ACT.Sqrt)

        gain_bank = gain_psum.tile([P, E], BF16)
        for c0 in range(0, E, BANK):
            nc.tensor.matmul(
                out=gain_bank[:, c0 : c0 + BANK],
                lhsT=ones[:],
                rhs=gain_row[:, c0 : c0 + BANK],
                start=True,
                stop=True,
            )

        gpsimd_gain = const.tile([P, GPSIMD_MAX], BF16)

        def gain_for_gpsimd():
            nc.vector.tensor_copy(
                out=gpsimd_gain[:, : GPSIMD_MAX - E], in_=gain_bank[:, 2 * E - GPSIMD_MAX :]
            )
            nc.vector.tensor_copy(out=gpsimd_gain[:, GPSIMD_MAX - E :], in_=gain_bank[:])

        w_grouped = const.tile([P, PASSES, COLS, PACK], BF16, align_bytes=64)
        w_codes = const.tile([P, PASSES, COLS], U32, align_bytes=64)
        w_scales = const.tile([P, PASSES, COLS], U8, align_bytes=64)

        def regroup_weights(g, on_gpsimd):
            by_part = w_raw[:, g].rearrange("p t (h s d) -> p s h d t", h=HEADS, s=PARTS)
            for s in range(PARTS):
                out = w_grouped[:, g, s * PART_COLS : (s + 1) * PART_COLS, :].rearrange(
                    "p (h d) t -> p h d t", h=HEADS
                )
                if on_gpsimd:
                    nc.gpsimd.tensor_scalar(
                        out=out, in0=by_part[:, s], scalar1=1.0, scalar2=0.0, op0=ALU.mult, op1=ALU.add
                    )
                else:
                    nc.vector.tensor_copy(out=out, in_=by_part[:, s])

        def quantise_weights():
            for g in range(PASSES):
                for c0, c1 in COLUMN_CUTS:
                    nc.vector.quantize_mx(
                        out=w_codes[:, g, c0:c1].bitcast(FP8X4),
                        scales=w_scales[:, g, c0:c1],
                        in_=w_grouped[:, g, c0:c1, :].rearrange("p c t -> p (c t)"),
                    )

        sum_sq_of, rms_of, rstd_of, xn_of, turned_of = {}, {}, {}, {}, {}
        grouped_of, codes_of, scales_of, acc_of, result_of = {}, {}, {}, {}, {}
        scaled_of = {}

        def start_statistics(n):
            sum_sq_of[n] = stat_pool.tile([P, TILES], F32, name="sum_sq")
            rms_of[n] = stat_pool.tile([P, TILES], F32, name="rms")
            rstd_of[n] = stat_pool.tile([P, TILES], F32, name="rstd")

        def square_tile(n, j):
            squares = square_pool.tile([P, E], BF16, name="squares")
            nc.scalar.activation(
                out=squares[:],
                in_=x_tiles[n][:, j, :],
                func=ACT.Square,
                accum_out=sum_sq_of[n][:, j : j + 1],
            )

        def vector_square(n, j):
            squares = const.tile([P, E], F32, name="vector_squares")
            nc.vector.scalar_tensor_tensor(
                out=squares[:],
                in0=x_tiles[n][:, j, :],
                scalar=1.0,
                in1=x_tiles[n][:, j, :],
                op0=ALU.mult,
                op1=ALU.mult,
                accum_out=sum_sq_of[n][:, j : j + 1],
            )

        def gpsimd_scale(n):
            cols = gpsimd_cols(n)
            scaled = work.tile([P, GPSIMD_MAX], F32, name="scaled")
            nc.gpsimd.tensor_tensor(
                out=scaled[:, :cols],
                in0=x_tiles[n][:].rearrange("p j e -> p (j e)")[:, TILES * E - cols :],
                in1=gpsimd_gain[:, GPSIMD_MAX - cols :],
                op=ALU.mult,
            )
            scaled_of[n] = scaled

        def gpsimd_normalise(n):
            cols = gpsimd_cols(n)
            for j in range(TILES):
                first = vector_share(n, j)
                if first < E:
                    start = j * E + first - (TILES * E - cols)
                    nc.gpsimd.tensor_scalar(
                        out=xn_of[n][:, j, first:],
                        in0=scaled_of[n][:, start : start + E - first],
                        scalar1=rstd_of[n][:, j : j + 1],
                        scalar2=0.0,
                        op0=ALU.mult,
                        op1=ALU.add,
                    )

        def root(n, first, tiles):
            nc.scalar.activation(
                out=rms_of[n][:, first : first + tiles],
                in_=sum_sq_of[n][:, first : first + tiles],
                func=ACT.Sqrt,
                scale=1.0 / E,
                bias=EPS,
            )

        def invert(n, first=0, tiles=TILES):
            nc.vector.reciprocal(
                rstd_of[n][:, first : first + tiles], rms_of[n][:, first : first + tiles]
            )

        def start_group(n):
            xn_of[n] = work.tile([P, TILES, E], BF16, name="xn")
            grouped_of[n] = work.tile(
                [P, TILES, PASSES, P, PACK], BF16, align_bytes=64, name="grouped"
            )

        def normalise(n, j):
            share = vector_share(n, j)
            if share > 0:
                nc.vector.scalar_tensor_tensor(
                    out=xn_of[n][:, j, :share],
                    in0=x_tiles[n][:, j, :share],
                    scalar=rstd_of[n][:, j : j + 1],
                    in1=gain_bank[:, :share],
                    op0=ALU.mult,
                    op1=ALU.mult,
                )

        def turn(n, j):
            turned = turned_psum.tile([P, BLOCKS, P], F32, name="turned")
            words = xn_of[n][:].bitcast(F32)
            for b in range(BLOCKS):
                nc.tensor.transpose(turned[:, b, :], words[:, j, b * P : (b + 1) * P], ident[:])
            turned_of[n, j] = turned

        def copy_turned(n, j, copy):
            copy(
                out=grouped_of[n][:].bitcast(F32)[:, j],
                in_=turned_of[n, j][:].rearrange("p (g u) r -> p g r u", u=2),
            )

        def quantise(n, first=0, tiles=TILES):
            if first == 0:
                codes_of[n] = work.tile([P, TILES, PASSES, P], U32, align_bytes=64, name="codes")
                scales_of[n] = work.tile([P, TILES, PASSES, P], U8, align_bytes=64, name="scales")
            last = first + tiles
            nc.vector.quantize_mx(
                out=codes_of[n][:, first:last].rearrange("p j g r -> p (j g r)").bitcast(FP8X4),
                scales=scales_of[n][:, first:last].rearrange("p j g r -> p (j g r)"),
                in_=grouped_of[n][:, first:last].rearrange("p j g r t -> p (j g r t)"),
            )

        def multiply(n, j, c0, c1, out):
            for g in range(PASSES):
                nc.tensor.matmul_mx(
                    out=out,
                    lhsT=codes_of[n][:, j, g, :].bitcast(FP8X4),
                    lhsT_scale=scales_of[n][:, j, g, :],
                    rhs=w_codes[:, g, c0:c1].bitcast(FP8X4),
                    rhs_scale=w_scales[:, g, c0:c1],
                    start=(g == 0),
                    stop=(g == PASSES - 1),
                )

        def project(n, bank):
            if bank < 2:
                acc = acc_psum.tile([P, 2, QK_COLS], F32, name="acc")
                for i in range(2):
                    multiply(n, 2 * bank + i, 0, QK_COLS, acc[:, i, :])
            else:
                acc = acc_psum.tile([P, TILES, PART_COLS], F32, name="acc")
                for j in range(TILES):
                    multiply(n, j, QK_COLS, COLS, acc[:, j, :])
            acc_of[n, bank] = acc

        def start_result(n):
            result_of[n] = out_pool.tile([P, PARTS, TILES, PART_COLS], F32, name="result")

        def copy_bank(n, bank, copy):
            if bank < 2:
                copy(
                    out=result_of[n][:, 0:2, 2 * bank : 2 * bank + 2, :],
                    in_=acc_of[n, bank][:].rearrange("p j (s c) -> p s j c", s=2),
                )
            else:
                copy(out=result_of[n][:, 2], in_=acc_of[n, bank][:])

        def store(n, first=0, tiles=TILES):
            c0, c1 = first * PART_COLS, (first + tiles) * PART_COLS
            for s in range(PARTS):
                nc.sync.dma_start(
                    out=out_groups[s][n][:, c0:c1],
                    in_=result_of[n][:, s, first : first + tiles].rearrange("p j c -> p (j c)"),
                )

        def project_tile(n, j):
            acc = turned_psum.tile([P, COLS], F32, name="turned")
            for c0, c1 in COLUMN_CUTS:
                multiply(n, j, c0, c1, acc[:, c0:c1])
            acc_of[n, "tile", j] = acc

        def copy_tile(n, j, copy):
            copy(
                out=result_of[n][:, :, j, :],
                in_=acc_of[n, "tile", j][:].rearrange("p (s c) -> p s c", s=PARTS),
            )

        VB = TILES - 1
        for n in (0, 1):
            start_statistics(n)
        vector_square(0, 1)
        order = (0, 2, 3)
        done = [1]
        for j in order:
            square_tile(0, j)
            root(0, {0: 0, 2: 1, 3: 2}[j], 1)
        square_tile(1, 0)
        root(0, 3, 1)
        for j in range(1, TILES):
            square_tile(1, j)
        root(1, 0, TILES)
        start_group(0)
        for j in range(TILES):
            invert(0, j, 1)
            normalise(0, j)
            turn(0, j)
            if j == 9:
                gain_for_gpsimd()
        regroup_weights(0, True)
        regroup_weights(1, True)
        quantise_weights()
        gain_for_gpsimd()
        invert(1)
        gpsimd_scale(1)
        start_statistics(2)
        for j in range(TILES):
            square_tile(2, j)
        for r in range(1, LAST):
            old = r >= 2
            start_group(r)
            if old:
                start_result(r - 2)
            if r > 1:
                copy_turned(r - 1, VB, vec)
            gpsimd_normalise(r)
            for j in range(TILES):
                normalise(r, j)
                if r == 1:
                    copy_turned(0, j, vec)
                turn(r, j)
                if old and j == 0:
                    project(r - 2, 2)
            copy_turned(r, 0, sca)
            root(r + 1, 0, TILES)
            if old:
                for bank in range(BANKS):
                    copy_bank(r - 2, bank, vec if r < LAST - 1 else sca)
                store(r - 2)
            quantise(r - 1)
            invert(r + 1)
            gpsimd_scale(r + 1)
            if r + 2 < GROUPS:
                start_statistics(r + 2)
            for j in range(TILES):
                if 1 <= j < VB:
                    copy_turned(r, j, sca)
                if r + 2 < GROUPS:
                    square_tile(r + 2, j)
            project(r - 1, 0)
            project(r - 1, 1)
        n = LAST
        start_group(n)
        start_result(n - 2)
        gpsimd_normalise(n)
        copy_turned(n - 1, VB, sca)
        normalise(n, 0)
        turn(n, 0)
        project(n - 2, 2)
        copy_bank(n - 2, 0, sca)
        copy_bank(n - 2, 1, sca)
        copy_turned(n, 0, sca)
        normalise(n, 1)
        turn(n, 1)
        copy_turned(n, 1, sca)
        quantise(n - 1)
        normalise(n, 3)
        turn(n, 3)
        start_result(n - 1)
        project(n - 1, 0)
        copy_turned(n, 3, sca)
        copy_bank(n - 2, 2, sca)
        store(n - 2)
        normalise(n, 2)
        turn(n, 2)
        project(n - 1, 1)
        project(n - 1, 2)
        copy_turned(n, 2, sca)
        quantise(n, 0, 1)
        project_tile(n, 0)
        quantise(n, 1, 1)
        project_tile(n, 1)
        copy_bank(n - 1, 0, vec)
        quantise(n, 3, 1)
        project_tile(n, 3)
        quantise(n, 2, 1)
        copy_bank(n - 1, 1, sca)
        copy_bank(n - 1, 2, sca)
        store(n - 1)
        start_result(n)
        project_tile(n, 2)
        copy_tile(n, 0, vec)
        copy_tile(n, 1, sca)
        store(n, 0, 2)
        copy_tile(n, 3, vec)
        copy_tile(n, 2, sca)
        store(n, 2, 2)
